import numpy as np
import ml_dtypes

BF16 = ml_dtypes.bfloat16


def bf(x):
    return np.asarray(x, np.float32).astype(BF16)


def f32(x):
    return np.asarray(x, np.float32)


def f64(x):
    return np.asarray(x).astype(np.float64)


def striped(idx):
    return np.tile(idx.reshape(-1, 16).T, (8, 1))


C, S, N, F = 256, 4096, 512, 256
P_EDGE = 0.01


def setup_inputs():
    return {
        "base": f32(np.random.standard_normal((C, S))),
        "x": bf(np.random.standard_normal((F, N))),
        "w": bf(np.random.standard_normal((F, C)) / np.sqrt(F)),
        "adj_t": bf(np.random.random((N, N)) < P_EDGE),
        "b": f32(0.2 * np.random.standard_normal((C, 1))),
        "offs": striped(np.random.permutation(S)[:N]),
    }


def reference(base, x, w, adj_t, b, offs):
    idx = offs[:16].T.reshape(-1)
    y = f64(x).T @ f64(w)
    v = y.T @ f64(adj_t) + f64(b)
    m = (v > 0.0).astype(np.float64)
    out = f64(base).copy()
    out[:, idx] = v * m
    return out

@@ -1,0 +1,72 @@
+import concourse.mybir as mybir
+
+P = 128
+C, S, N, F = 256, 4096, 512, 256
+C_BLOCKS, F_BLOCKS, N_BLOCKS = C // P, F // P, N // P
+FLOPS = 2 * N * F * C + 2 * N * N * C
+
+BF16, F32, U16 = mybir.dt.bfloat16, mybir.dt.float32, mybir.dt.uint16
+MULT, IS_GT = mybir.AluOpType.mult, mybir.AluOpType.is_gt
+IDENTITY = mybir.ActivationFunctionType.Identity
+
+
+def tile_gtransformerblock_kernel(tc, base, x, w, adj_t, b, offs, out):
+    nc = tc.nc
+    with (
+        tc.tile_pool(name="held", bufs=1) as held,
+        tc.psum_pool(name="psum", bufs=1) as psum,
+    ):
+        offsets = held.tile([P, N // 16], U16, name="offsets")
+        nc.sync.dma_start(offsets[:], offs)
+        x_sb = held.tile([P, F_BLOCKS, N], BF16, name="x_sb")
+        nc.sync.dma_start(x_sb[:], x.rearrange("(k p) i -> p k i", p=P))
+        w_sb = held.tile([P, F_BLOCKS, C], BF16, name="w_sb")
+        nc.sync.dma_start(w_sb[:], w.rearrange("(k p) c -> p k c", p=P))
+        adj_sb = held.tile([P, N_BLOCKS, N], BF16, name="adj_sb")
+        nc.sync.dma_start(adj_sb[:], adj_t.rearrange("(k p) j -> p k j", p=P))
+        bias = [held.tile([P, 1], F32, name=f"bias{cb}") for cb in range(C_BLOCKS)]
+        for cb in range(C_BLOCKS):
+            nc.scalar.dma_start(bias[cb][:], b[cb * P : (cb + 1) * P, :])
+        window = [held.tile([P, S], F32, name=f"window{cb}") for cb in range(C_BLOCKS)]
+        for cb in range(C_BLOCKS):
+            nc.sync.dma_start(window[cb][:], base[cb * P : (cb + 1) * P, :])
+
+        y_sb = [held.tile([P, 2, C], BF16, name=f"y_sb{h}") for h in range(N_BLOCKS // 2)]
+        for h in range(N_BLOCKS // 2):
+            y_ps = psum.tile([P, 2, C], F32, name=f"y_ps{h}")
+            for t in range(2):
+                ib = 2 * h + t
+                for fb in range(F_BLOCKS):
+                    nc.tensor.matmul(
+                        y_ps[:, t, :],
+                        x_sb[:, fb, ib * P : (ib + 1) * P],
+                        w_sb[:, fb, :],
+                        start=(fb == 0),
+                        stop=(fb == F_BLOCKS - 1),
+                    )
+            if h == 0:
+                nc.vector.tensor_copy(y_sb[h][:], y_ps[:])
+            else:
+                nc.scalar.copy(y_sb[h][:], y_ps[:])
+
+        v_sb, m_sb = [], []
+        for cb in range(C_BLOCKS):
+            v_ps = psum.tile([P, N], F32, name=f"v_ps{cb}")
+            for ib in range(N_BLOCKS):
+                nc.tensor.matmul(
+                    v_ps[:],
+                    y_sb[ib // 2][:, ib % 2, cb * P : (cb + 1) * P],
+                    adj_sb[:, ib, :],
+                    start=(ib == 0),
+                    stop=(ib == N_BLOCKS - 1),
+                )
+            v = held.tile([P, N], F32, name=f"v{cb}")
+            nc.scalar.activation(v[:], v_ps[:], IDENTITY, bias=bias[cb][:])
+            m = held.tile([P, N], F32, name=f"m{cb}")
+            nc.vector.tensor_single_scalar(m[:], v[:], 0.0, IS_GT)
+            v_sb.append(v)
+            m_sb.append(m)
+
+        for cb in range(C_BLOCKS):
+            nc.vector.tensor_tensor(window[cb][:].indirect(offsets[:]), v_sb[cb][:], m_sb[cb][:], MULT)
+            nc.sync.dma_start(out[cb * P : (cb + 1) * P, :], window[cb][:])

@@ -19,11 +19,11 @@ def tile_gtransformerblock_kernel(tc, base, x, w, adj_t, b, offs, out):
         offsets = held.tile([P, N // 16], U16, name="offsets")
         nc.sync.dma_start(offsets[:], offs)
         x_sb = held.tile([P, F_BLOCKS, N], BF16, name="x_sb")
-        nc.sync.dma_start(x_sb[:], x.rearrange("(k p) i -> p k i", p=P))
+        nc.sync.dma_start(x_sb[:], x.rearrange("(p k) i -> p k i", p=P))
         w_sb = held.tile([P, F_BLOCKS, C], BF16, name="w_sb")
-        nc.sync.dma_start(w_sb[:], w.rearrange("(k p) c -> p k c", p=P))
+        nc.sync.dma_start(w_sb[:], w.rearrange("(p k) c -> p k c", p=P))
         adj_sb = held.tile([P, N_BLOCKS, N], BF16, name="adj_sb")
-        nc.sync.dma_start(adj_sb[:], adj_t.rearrange("(k p) j -> p k j", p=P))
+        nc.sync.dma_start(adj_sb[:], adj_t.rearrange("(p k) j -> p k j", p=P))
         bias = [held.tile([P, 1], F32, name=f"bias{cb}") for cb in range(C_BLOCKS)]
         for cb in range(C_BLOCKS):
             nc.scalar.dma_start(bias[cb][:], b[cb * P : (cb + 1) * P, :])
@@ -39,7 +39,7 @@ def tile_gtransformerblock_kernel(tc, base, x, w, adj_t, b, offs, out):
                 for fb in range(F_BLOCKS):
                     nc.tensor.matmul(
                         y_ps[:, t, :],
-                        x_sb[:, fb, ib * P : (ib + 1) * P],
+                        x_sb[:, fb, ib : N : N_BLOCKS],
                         w_sb[:, fb, :],
                         start=(fb == 0),
                         stop=(fb == F_BLOCKS - 1),
@@ -49,7 +49,6 @@ def tile_gtransformerblock_kernel(tc, base, x, w, adj_t, b, offs, out):
             else:
                 nc.scalar.copy(y_sb[h][:], y_ps[:])
 
-        v_sb, m_sb = [], []
         for cb in range(C_BLOCKS):
             v_ps = psum.tile([P, N], F32, name=f"v_ps{cb}")
             for ib in range(N_BLOCKS):
@@ -64,9 +63,5 @@ def tile_gtransformerblock_kernel(tc, base, x, w, adj_t, b, offs, out):
             nc.scalar.activation(v[:], v_ps[:], IDENTITY, bias=bias[cb][:])
             m = held.tile([P, N], F32, name=f"m{cb}")
             nc.vector.tensor_single_scalar(m[:], v[:], 0.0, IS_GT)
-            v_sb.append(v)
-            m_sb.append(m)
-
-        for cb in range(C_BLOCKS):
-            nc.vector.tensor_tensor(window[cb][:].indirect(offsets[:]), v_sb[cb][:], m_sb[cb][:], MULT)
+            nc.vector.tensor_tensor(window[cb][:].indirect(offsets[:]), v[:], m[:], MULT)
             nc.sync.dma_start(out[cb * P : (cb + 1) * P, :], window[cb][:])

@@ -14,6 +14,7 @@ def tile_gtransformerblock_kernel(tc, base, x, w, adj_t, b, offs, out):
     nc = tc.nc
     with (
         tc.tile_pool(name="held", bufs=1) as held,
+        tc.tile_pool(name="single", bufs=1) as single,
         tc.psum_pool(name="psum", bufs=1) as psum,
     ):
         offsets = held.tile([P, N // 16], U16, name="offsets")
@@ -61,7 +62,7 @@ def tile_gtransformerblock_kernel(tc, base, x, w, adj_t, b, offs, out):
                 )
             v = held.tile([P, N], F32, name=f"v{cb}")
             nc.scalar.activation(v[:], v_ps[:], IDENTITY, bias=bias[cb][:])
-            m = held.tile([P, N], F32, name=f"m{cb}")
+            m = single.tile([P, N], F32, name="m")
             nc.vector.tensor_single_scalar(m[:], v[:], 0.0, IS_GT)
             nc.vector.tensor_tensor(window[cb][:].indirect(offsets[:]), v[:], m[:], MULT)
             nc.sync.dma_start(out[cb * P : (cb + 1) * P, :], window[cb][:])

@@ -51,7 +51,7 @@ def tile_gtransformerblock_kernel(tc, base, x, w, adj_t, b, offs, out):
                 nc.scalar.copy(y_sb[h][:], y_ps[:])
 
         for cb in range(C_BLOCKS):
-            v_ps = psum.tile([P, N], F32, name=f"v_ps{cb}")
+            v_ps = psum.tile([P, N], F32, name="v_ps")
             for ib in range(N_BLOCKS):
                 nc.tensor.matmul(
                     v_ps[:],

@@ -3,6 +3,7 @@ import concourse.mybir as mybir
 P = 128
 C, S, N, F = 256, 4096, 512, 256
 C_BLOCKS, F_BLOCKS, N_BLOCKS = C // P, F // P, N // P
+HALF = S // 2
 FLOPS = 2 * N * F * C + 2 * N * N * C
 
 BF16, F32, U16 = mybir.dt.bfloat16, mybir.dt.float32, mybir.dt.uint16
@@ -30,7 +31,9 @@ def tile_gtransformerblock_kernel(tc, base, x, w, adj_t, b, offs, out):
             nc.scalar.dma_start(bias[cb][:], b[cb * P : (cb + 1) * P, :])
         window = [held.tile([P, S], F32, name=f"window{cb}") for cb in range(C_BLOCKS)]
         for cb in range(C_BLOCKS):
-            nc.sync.dma_start(window[cb][:], base[cb * P : (cb + 1) * P, :])
+            for half in range(2):
+                cols = slice(half * HALF, (half + 1) * HALF)
+                nc.sync.dma_start(window[cb][:, cols], base[cb * P : (cb + 1) * P, cols])
 
         y_sb = [held.tile([P, 2, C], BF16, name=f"y_sb{h}") for h in range(N_BLOCKS // 2)]
         for h in range(N_BLOCKS // 2):
@@ -65,4 +68,6 @@ def tile_gtransformerblock_kernel(tc, base, x, w, adj_t, b, offs, out):
             m = single.tile([P, N], F32, name="m")
             nc.vector.tensor_single_scalar(m[:], v[:], 0.0, IS_GT)
             nc.vector.tensor_tensor(window[cb][:].indirect(offsets[:]), v[:], m[:], MULT)
-            nc.sync.dma_start(out[cb * P : (cb + 1) * P, :], window[cb][:])
+            for half in range(2):
+                cols = slice(half * HALF, (half + 1) * HALF)
+                nc.sync.dma_start(out[cb * P : (cb + 1) * P, cols], window[cb][:, cols])

@@ -9,13 +9,13 @@ FLOPS = 2 * N * F * C + 2 * N * N * C
 BF16, F32, U16 = mybir.dt.bfloat16, mybir.dt.float32, mybir.dt.uint16
 MULT, IS_GT = mybir.AluOpType.mult, mybir.AluOpType.is_gt
 IDENTITY = mybir.ActivationFunctionType.Identity
+SIGN, RELU = mybir.ActivationFunctionType.Sign, mybir.ActivationFunctionType.Relu
 
 
 def tile_gtransformerblock_kernel(tc, base, x, w, adj_t, b, offs, out):
     nc = tc.nc
     with (
         tc.tile_pool(name="held", bufs=1) as held,
-        tc.tile_pool(name="single", bufs=1) as single,
         tc.psum_pool(name="psum", bufs=1) as psum,
     ):
         offsets = held.tile([P, N // 16], U16, name="offsets")
@@ -65,8 +65,13 @@ def tile_gtransformerblock_kernel(tc, base, x, w, adj_t, b, offs, out):
                 )
             v = held.tile([P, N], F32, name=f"v{cb}")
             nc.scalar.activation(v[:], v_ps[:], IDENTITY, bias=bias[cb][:])
-            m = single.tile([P, N], F32, name="m")
-            nc.vector.tensor_single_scalar(m[:], v[:], 0.0, IS_GT)
+            m = held.tile([P, N], F32, name=f"m{cb}")
+            if cb == 0:
+                nc.vector.tensor_single_scalar(m[:], v[:], 0.0, IS_GT)
+            else:
+                sign = held.tile([P, N], F32, name="sign")
+                nc.scalar.activation(sign[:], v[:], SIGN)
+                nc.scalar.activation(m[:], sign[:], RELU)
             nc.vector.tensor_tensor(window[cb][:].indirect(offsets[:]), v[:], m[:], MULT)
             for half in range(2):
                 cols = slice(half * HALF, (half + 1) * HALF)

@@ -4,6 +4,7 @@ P = 128
 C, S, N, F = 256, 4096, 512, 256
 C_BLOCKS, F_BLOCKS, N_BLOCKS = C // P, F // P, N // P
 HALF = S // 2
+ALIGN = 4096
 FLOPS = 2 * N * F * C + 2 * N * N * C
 
 BF16, F32, U16 = mybir.dt.bfloat16, mybir.dt.float32, mybir.dt.uint16
@@ -20,16 +21,16 @@ def tile_gtransformerblock_kernel(tc, base, x, w, adj_t, b, offs, out):
     ):
         offsets = held.tile([P, N // 16], U16, name="offsets")
         nc.sync.dma_start(offsets[:], offs)
-        x_sb = held.tile([P, F_BLOCKS, N], BF16, name="x_sb")
+        x_sb = held.tile([P, F_BLOCKS, N], BF16, name="x_sb", align_bytes=ALIGN)
         nc.sync.dma_start(x_sb[:], x.rearrange("(p k) i -> p k i", p=P))
-        w_sb = held.tile([P, F_BLOCKS, C], BF16, name="w_sb")
+        w_sb = held.tile([P, F_BLOCKS, C], BF16, name="w_sb", align_bytes=ALIGN)
         nc.sync.dma_start(w_sb[:], w.rearrange("(p k) c -> p k c", p=P))
-        adj_sb = held.tile([P, N_BLOCKS, N], BF16, name="adj_sb")
+        adj_sb = held.tile([P, N_BLOCKS, N], BF16, name="adj_sb", align_bytes=ALIGN)
         nc.sync.dma_start(adj_sb[:], adj_t.rearrange("(p k) j -> p k j", p=P))
         bias = [held.tile([P, 1], F32, name=f"bias{cb}") for cb in range(C_BLOCKS)]
         for cb in range(C_BLOCKS):
             nc.scalar.dma_start(bias[cb][:], b[cb * P : (cb + 1) * P, :])
-        window = [held.tile([P, S], F32, name=f"window{cb}") for cb in range(C_BLOCKS)]
+        window = [held.tile([P, S], F32, name=f"window{cb}", align_bytes=ALIGN) for cb in range(C_BLOCKS)]
         for cb in range(C_BLOCKS):
             for half in range(2):
                 cols = slice(half * HALF, (half + 1) * HALF)

import concourse.mybir as mybir

P = 128
C, S, N, F = 256, 4096, 512, 256
C_BLOCKS, F_BLOCKS, N_BLOCKS = C // P, F // P, N // P
HALF = S // 2
ALIGN = 4096
FLOPS = 2 * N * F * C + 2 * N * N * C

BF16, F32, U16 = mybir.dt.bfloat16, mybir.dt.float32, mybir.dt.uint16
MULT, IS_GT = mybir.AluOpType.mult, mybir.AluOpType.is_gt
IDENTITY = mybir.ActivationFunctionType.Identity
SIGN, RELU = mybir.ActivationFunctionType.Sign, mybir.ActivationFunctionType.Relu


def tile_gtransformerblock_kernel(tc, base, x, w, adj_t, b, offs, out):
    nc = tc.nc
    with (
        tc.tile_pool(name="held", bufs=1) as held,
        tc.psum_pool(name="psum", bufs=1) as psum,
    ):
        offsets = held.tile([P, N // 16], U16, name="offsets")
        nc.sync.dma_start(offsets[:], offs)
        x_sb = held.tile([P, F_BLOCKS, N], BF16, name="x_sb", align_bytes=ALIGN)
        nc.sync.dma_start(x_sb[:], x.rearrange("(p k) i -> p k i", p=P))
        w_sb = held.tile([P, F_BLOCKS, C], BF16, name="w_sb", align_bytes=ALIGN)
        nc.sync.dma_start(w_sb[:], w.rearrange("(p k) c -> p k c", p=P))
        adj_sb = held.tile([P, N_BLOCKS, N], BF16, name="adj_sb", align_bytes=ALIGN)
        nc.sync.dma_start(adj_sb[:], adj_t.rearrange("(p k) j -> p k j", p=P))
        bias = [held.tile([P, 1], F32, name=f"bias{cb}") for cb in range(C_BLOCKS)]
        for cb in range(C_BLOCKS):
            nc.scalar.dma_start(bias[cb][:], b[cb * P : (cb + 1) * P, :])
        window = [held.tile([P, S], F32, name=f"window{cb}", align_bytes=ALIGN) for cb in range(C_BLOCKS)]
        for cb in range(C_BLOCKS):
            for half in range(2):
                cols = slice(half * HALF, (half + 1) * HALF)
                nc.sync.dma_start(window[cb][:, cols], base[cb * P : (cb + 1) * P, cols])

        y_sb = [held.tile([P, 2, C], BF16, name=f"y_sb{h}") for h in range(N_BLOCKS // 2)]
        for h in range(N_BLOCKS // 2):
            y_ps = psum.tile([P, 2, C], F32, name=f"y_ps{h}")
            for t in range(2):
                ib = 2 * h + t
                for fb in range(F_BLOCKS):
                    nc.tensor.matmul(
                        y_ps[:, t, :],
                        x_sb[:, fb, ib : N : N_BLOCKS],
                        w_sb[:, fb, :],
                        start=(fb == 0),
                        stop=(fb == F_BLOCKS - 1),
                    )
            if h == 0:
                nc.vector.tensor_copy(y_sb[h][:], y_ps[:])
            else:
                nc.scalar.copy(y_sb[h][:], y_ps[:])

        for cb in range(C_BLOCKS):
            v_ps = psum.tile([P, N], F32, name="v_ps")
            for ib in range(N_BLOCKS):
                nc.tensor.matmul(
                    v_ps[:],
                    y_sb[ib // 2][:, ib % 2, cb * P : (cb + 1) * P],
                    adj_sb[:, ib, :],
                    start=(ib == 0),
                    stop=(ib == N_BLOCKS - 1),
                )
            v = held.tile([P, N], F32, name=f"v{cb}")
            nc.scalar.activation(v[:], v_ps[:], IDENTITY, bias=bias[cb][:])
            m = held.tile([P, N], F32, name=f"m{cb}")
            if cb == 0:
                nc.vector.tensor_single_scalar(m[:], v[:], 0.0, IS_GT)
            else:
                sign = held.tile([P, N], F32, name="sign")
                nc.scalar.activation(sign[:], v[:], SIGN)
                nc.scalar.activation(m[:], sign[:], RELU)
            nc.vector.tensor_tensor(window[cb][:].indirect(offsets[:]), v[:], m[:], MULT)
            for half in range(2):
                cols = slice(half * HALF, (half + 1) * HALF)
                nc.sync.dma_start(out[cb * P : (cb + 1) * P, cols], window[cb][:, cols])
